import numpy as np
import ml_dtypes


def mxq(x, axis, fmt="e4m3"):
    dtype, down = {"e4m3": (ml_dtypes.float8_e4m3fn, 7), "e5m2": (ml_dtypes.float8_e5m2, 14)}[fmt]
    v = np.moveaxis(np.asarray(x, np.float32).astype(ml_dtypes.bfloat16).astype(np.float64), axis, -1)
    blocks = v.reshape(v.shape[:-1] + (-1, 32))
    amax = np.abs(blocks).max(-1, keepdims=True)
    byte = np.maximum(np.where(amax > 0, np.frexp(amax)[1] - 1 + 127, 0) - down, 1)
    scale = np.exp2(byte - 127.0)
    codes = (blocks / scale).astype(np.float32).astype(dtype).astype(np.float64)
    return np.moveaxis((codes * scale).reshape(v.shape), -1, axis)


WIDE = False


def mx_kscale(k):
    if not WIDE:
        return np.ones(k)
    levels = np.array([10, -10, 5, -5, 0])
    a = np.random.permutation(np.resize(levels, k // 512 * 4)).reshape(k // 512, 4)
    idx = np.arange(k)
    return np.exp2(a[idx // 512, idx % 128 // 32])


BF16 = ml_dtypes.bfloat16


def bf(x):
    return np.asarray(x, np.float32).astype(BF16)


def f64(x):
    return np.asarray(x).astype(np.float64)


B, S, D, K, O, DEG, BLK = 4, 1024, 1024, 1024, 2048, 4, 512
HALF = DEG // 2
STEP = K // DEG


def make_masks(lo, hi):
    rows = np.arange(K)
    deg_r = (rows * DEG) // K + 1
    degmask = (np.arange(1, DEG + 1)[:, None] <= deg_r[None, :]) * 1.0
    tri_l = np.tril(np.ones((K, D)))
    tri_u = np.triu(np.ones((K, D)))
    return np.stack([degmask[i][:, None] * (tri_l if i % 2 == 0 else tri_u) for i in range(lo, hi)])


def factor(zq, Wi, i):
    y = np.zeros((zq.shape[0], K))
    for j in range(K // BLK):
        a, b = max(j * BLK, i * STEP), (j + 1) * BLK
        c0, c1 = (0, min(b, D)) if i % 2 == 0 else (j * BLK, D)
        if a >= b or c0 >= c1:
            continue
        y[:, a:b] = zq[:, c0:c1] @ mxq(Wi[a:b, c0:c1], 1, "e4m3").T
    return y


def setup_inputs():
    s = mx_kscale(D)
    return {"z": bf(np.random.standard_normal((B, S, D)) * s),
            "U_lo": bf(np.random.standard_normal((HALF, K, D)) / np.sqrt(D) / s),
            "masks_lo": bf(make_masks(0, HALF))}


def reference(z, U_lo, masks_lo):
    zq = mxq(f64(z).reshape(-1, D), 1, "e4m3")
    W = f64(masks_lo) * f64(U_lo)
    out = factor(zq, W[0], 0)
    for i in range(1, HALF):
        out = factor(zq, W[i], i) * out + out
    return out

@@ -1,0 +1,295 @@
+from contextlib import ExitStack
+
+import concourse.mybir as mybir
+from concourse.masks import make_identity
+
+F32 = mybir.dt.float32
+BF16 = mybir.dt.bfloat16
+U32 = mybir.dt.uint32
+U8 = mybir.dt.uint8
+FP8X4 = mybir.dt.float8_e4m3fn_x4
+ALU = mybir.AluOpType
+
+P = 128
+TOKENS = 4096
+FEATS = 1024
+RANKS = 1024
+GROUP = 4
+N_GROUPS = TOKENS // (P * GROUP)
+
+FLOPS = 2 * TOKENS * 1310720
+BYTES = TOKENS * FEATS * 2 + TOKENS * RANKS * 4 + 2 * 1310720 * 2
+
+GENERAL = True
+PIN = True
+ZCOPY = "svsv"
+WCOPY = "svsvsvsvsv"
+OUT_BUFS = 6
+
+
+def spec_range(i, rp):
+    if i == 0:
+        return (0, 512) if rp < 2 else (0, 1024)
+    return (0, 1024) if rp == 1 else (512, 1024)
+
+
+def live_range(i, rp):
+    if GENERAL:
+        return spec_range(i, rp)
+    return (0, 256 * (rp + 1)) if i == 0 else (256 * rp, 1024)
+
+
+def mask_range(i, rp):
+    if GENERAL:
+        return spec_range(i, rp)
+    return (256 * rp, 256 * rp + 256)
+
+
+def tile_cp_sparse_degree_lu_pa_t_kernel(tc, z, U_lo, masks_lo, out):
+    nc = tc.nc
+    zf = z.flatten_outer_dims()
+    with ExitStack() as ctx:
+        const = ctx.enter_context(tc.tile_pool(name="const", bufs=1))
+        zin = ctx.enter_context(tc.tile_pool(name="zin", bufs=N_GROUPS))
+        zwork = ctx.enter_context(tc.tile_pool(name="zwork", bufs=3))
+        outp = ctx.enter_context(tc.tile_pool(name="outp", bufs=OUT_BUFS))
+        psum = ctx.enter_context(tc.psum_pool(name="psum", bufs=8))
+        if PIN:
+            ctx.enter_context(tc.manual_schedule())
+
+        count = [0]
+
+        def bank():
+            count[0] += 1
+            return psum.tile([P, 512], F32, name="bank%d" % count[0], tag="bank")
+
+        def copy_out(eng, dst, src):
+            if eng == "s":
+                nc.scalar.copy(out=dst, in_=src)
+            else:
+                nc.vector.tensor_copy(out=dst, in_=src)
+
+        ident = const.tile([P, P], F32, name="ident")
+        make_identity(nc, ident[:])
+
+        pairs_a = [(0, 0), (0, 1), (1, 1)]
+        pairs_b = [(0, 2), (0, 3), (1, 2), (1, 3)]
+        raws = {}
+        msks = {}
+        for key in pairs_a + pairs_b:
+            i, rp = key
+            s0, s1 = spec_range(i, rp)
+            m0, m1 = mask_range(i, rp)
+            raws[key] = const.tile([P, 2 * (s1 - s0)], BF16, name="raw%d%d" % key)
+            msks[key] = const.tile([P, 2 * (m1 - m0)], BF16, name="msk%d%d" % key)
+            l0, l1 = live_range(i, rp)
+            r3 = raws[key][:].rearrange("p (r c) -> p r c", r=2)
+            if l0 > s0:
+                nc.vector.memset(r3[:, :, 0 : l0 - s0], 0.0)
+            if l1 < s1:
+                nc.vector.memset(r3[:, :, l1 - s0 : s1 - s0], 0.0)
+        wg = [const.tile([P, 2048], BF16, name="wg%d" % s, align_bytes=64) for s in range(5)]
+        wc = [const.tile([P, 512], U32, name="wc%d" % s, align_bytes=64) for s in range(5)]
+        ws = [const.tile([P, 512], U8, name="ws%d" % s, align_bytes=64) for s in range(5)]
+
+        def load_w(key):
+            i, rp = key
+            s0, s1 = spec_range(i, rp)
+            m0, m1 = mask_range(i, rp)
+            l0, l1 = live_range(i, rp)
+            rows = slice(256 * rp, 256 * rp + 256)
+            nc.sync.dma_start(
+                out=msks[key][:].rearrange("p (r c) -> p r c", r=2),
+                in_=masks_lo[i, rows, m0:m1].rearrange("(r p) c -> p r c", p=P),
+            )
+            nc.sync.dma_start(
+                out=raws[key][:].rearrange("p (r c) -> p r c", r=2)[:, :, l0 - s0 : l1 - s0],
+                in_=U_lo[i, rows, l0:l1].rearrange("(r p) c -> p r c", p=P),
+            )
+
+        zraw = [zin.tile([P, GROUP * FEATS], BF16, name="zraw%d" % g, tag="zraw") for g in range(N_GROUPS)]
+
+        def load_z(grp, j0, j1):
+            src = zf[512 * grp : 512 * grp + 512, :].rearrange("(p j) c -> p j c", j=GROUP)
+            dst = zraw[grp][:].rearrange("p (j c) -> p j c", j=GROUP)
+            nc.sync.dma_start(out=dst[:, j0:j1, :], in_=src[:, j0:j1, :])
+
+        for key in pairs_a:
+            load_w(key)
+        load_z(0, 0, 2)
+        load_z(0, 2, 4)
+        for key in pairs_b:
+            load_w(key)
+        for grp in range(1, N_GROUPS):
+            load_z(grp, 0, GROUP)
+
+        def mask_mult(key):
+            i, rp = key
+            s0, s1 = spec_range(i, rp)
+            m0, m1 = mask_range(i, rp)
+            part = raws[key][:].rearrange("p (r c) -> p r c", r=2)[:, :, m0 - s0 : m1 - s0]
+            nc.vector.tensor_tensor(
+                out=part, in0=part, in1=msks[key][:].rearrange("p (r c) -> p r c", r=2), op=ALU.mult
+            )
+
+        def w_bank(i, g, rp, s, half, eng):
+            s0, s1 = spec_range(i, rp)
+            words = (s1 - s0) // 2
+            rawf = raws[(i, rp)][:].bitcast(F32)
+            bk = bank()
+            for u in range(2):
+                for r in range(2):
+                    w0 = r * words + (512 * g + 256 * u - s0) // 2
+                    nc.tensor.transpose(
+                        out=bk[:, 256 * u + P * r : 256 * u + P * r + P], in_=rawf[:, w0 : w0 + P], identity=ident[:]
+                    )
+            copy_out(
+                eng,
+                wg[s][:].bitcast(F32)[:, 512 * half : 512 * half + 512].rearrange("p (r u) -> p r u", u=2),
+                bk[:].rearrange("p (u r) -> p r u", u=2),
+            )
+
+        def w_quant(s):
+            nc.vector.quantize_mx(out=wc[s][:].bitcast(FP8X4), scales=ws[s][:], in_=wg[s][:])
+
+        zg = {}
+        zc = {}
+        zs = {}
+
+        def z_tiles(grp):
+            zg[grp] = zwork.tile([P, GROUP * FEATS], BF16, name="zg%d" % grp, tag="zg", align_bytes=64)
+            zc[grp] = zwork.tile([P, GROUP * 256], U32, name="zc%d" % grp, tag="zc", align_bytes=64)
+            zs[grp] = zwork.tile([P, GROUP * 256], U8, name="zs%d" % grp, tag="zs", align_bytes=64)
+
+        def z_transposes(grp, js):
+            zrf = zraw[grp][:].bitcast(F32)
+            bks = []
+            for j in js:
+                bk = bank()
+                for c in range(4):
+                    nc.tensor.transpose(
+                        out=bk[:, P * c : P * c + P], in_=zrf[:, 512 * j + P * c : 512 * j + P * c + P], identity=ident[:]
+                    )
+                bks.append(bk)
+            for j, bk in zip(js, bks):
+                copy_out(
+                    ZCOPY[j],
+                    zg[grp][:].bitcast(F32)[:, 512 * j : 512 * j + 512].rearrange("p (g t u) -> p g t u", g=2, u=2),
+                    bk[:].rearrange("p (g u t) -> p g t u", g=2, u=2),
+                )
+
+        def z_quant(grp, h):
+            nc.vector.quantize_mx(
+                out=zc[grp][:, 512 * h : 512 * h + 512].bitcast(FP8X4),
+                scales=zs[grp][:, 512 * h : 512 * h + 512],
+                in_=zg[grp][:, 2048 * h : 2048 * h + 2048],
+            )
+
+        def mm(dst, grp, j, g, s, c0, c1, start, stop):
+            a = 256 * j + P * g
+            nc.tensor.matmul_mx(
+                out=dst,
+                lhsT=zc[grp][:, a : a + P].bitcast(FP8X4),
+                lhsT_scale=zs[grp][:, a : a + P],
+                rhs=wc[s][:, c0:c1].bitcast(FP8X4),
+                rhs_scale=ws[s][:, c0:c1],
+                start=start,
+                stop=stop,
+            )
+
+        osb = {}
+
+        def half_a(grp, h):
+            o = outp.tile([P, 2 * RANKS], F32, name="o%d%d" % (grp, h), tag="o")
+            osb[(grp, h)] = o
+            y0 = []
+            for jj in range(2):
+                bk = bank()
+                mm(bk[:], grp, 2 * h + jj, 0, 0, 0, 512, True, True)
+                y0.append(bk)
+            y1 = bank()
+            for jj in range(2):
+                mm(y1[:, 256 * jj : 256 * jj + 256], grp, 2 * h + jj, 0, 1, 0, 256, True, False)
+                mm(y1[:, 256 * jj : 256 * jj + 256], grp, 2 * h + jj, 1, 1, 256, 512, False, True)
+            for jj in range(2):
+                nc.scalar.copy(out=o[:, RANKS * jj : RANKS * jj + 512], in_=y0[jj][:])
+            o3 = o[:].rearrange("p (j r) -> p j r", j=2)[:, :, 256:512]
+            nc.vector.scalar_tensor_tensor(
+                out=o3, in0=y1[:].rearrange("p (j r) -> p j r", j=2), scalar=1.0, in1=o3, op0=ALU.add, op1=ALU.mult
+            )
+
+        def half_b(grp, h, fine):
+            o = osb[(grp, h)]
+            y0 = []
+            for jj in range(2):
+                bk = bank()
+                mm(bk[:], grp, 2 * h + jj, 0, 2, 0, 512, True, False)
+                mm(bk[:], grp, 2 * h + jj, 1, 3, 0, 512, False, True)
+                y0.append(bk)
+            y1 = []
+            for jj in range(2):
+                bk = bank()
+                mm(bk[:], grp, 2 * h + jj, 1, 4, 0, 512, True, True)
+                y1.append(bk)
+            for jj in range(2):
+                nc.scalar.copy(out=o[:, RANKS * jj + 512 : RANKS * jj + 1024], in_=y0[jj][:])
+            for jj in range(2):
+                part = o[:, RANKS * jj + 512 : RANKS * jj + 1024]
+                nc.vector.scalar_tensor_tensor(
+                    out=part, in0=y1[jj][:], scalar=1.0, in1=part, op0=ALU.add, op1=ALU.mult
+                )
+                if fine:
+                    store(grp, h, jj, jj + 1, 512, RANKS)
+            if not fine:
+                store(grp, h, 0, 2, 0, RANKS)
+
+        def store(grp, h, j0, j1, r0, r1):
+            dst = out[512 * grp : 512 * grp + 512, :].rearrange("(p j) r -> p j r", j=GROUP)
+            src = osb[(grp, h)][:].rearrange("p (j r) -> p j r", j=2)
+            nc.sync.dma_start(out=dst[:, 2 * h + j0 : 2 * h + j1, r0:r1], in_=src[:, j0:j1, r0:r1])
+
+        for key in pairs_a:
+            mask_mult(key)
+        w_bank(0, 0, 0, 0, 0, WCOPY[0])
+        w_bank(0, 0, 1, 0, 1, WCOPY[1])
+        w_bank(1, 0, 1, 1, 0, WCOPY[2])
+        w_bank(1, 1, 1, 1, 1, WCOPY[3])
+        w_quant(0)
+        z_tiles(0)
+        z_transposes(0, [0, 1])
+        w_quant(1)
+        z_transposes(0, [2, 3])
+        z_quant(0, 0)
+        z_quant(0, 1)
+        half_a(0, 0)
+        half_a(0, 1)
+        for key in pairs_b:
+            mask_mult(key)
+        w_bank(0, 0, 2, 2, 0, WCOPY[4])
+        w_bank(0, 0, 3, 2, 1, WCOPY[5])
+        w_bank(0, 1, 2, 3, 0, WCOPY[6])
+        w_bank(0, 1, 3, 3, 1, WCOPY[7])
+        w_quant(2)
+        w_bank(1, 1, 2, 4, 0, WCOPY[8])
+        w_bank(1, 1, 3, 4, 1, WCOPY[9])
+        w_quant(3)
+        z_tiles(1)
+        z_transposes(1, [0, 1, 2, 3])
+        w_quant(4)
+        z_quant(1, 0)
+        half_b(0, 0, False)
+        z_quant(1, 1)
+        half_b(0, 1, False)
+        for grp in range(1, N_GROUPS):
+            nxt = grp + 1
+            if nxt < N_GROUPS:
+                z_tiles(nxt)
+                z_transposes(nxt, [0, 1, 2, 3])
+            for h in range(2):
+                last = grp == N_GROUPS - 1 and h == 1
+                half_a(grp, h)
+                if last:
+                    store(grp, h, 0, 2, 0, 512)
+                half_b(grp, h, last)
+                if nxt < N_GROUPS:
+                    z_quant(nxt, h)

@@ -20,11 +20,23 @@ N_GROUPS = TOKENS // (P * GROUP)
 FLOPS = 2 * TOKENS * 1310720
 BYTES = TOKENS * FEATS * 2 + TOKENS * RANKS * 4 + 2 * 1310720 * 2
 
-GENERAL = True
+GENERAL = False
 PIN = True
 ZCOPY = "svsv"
-WCOPY = "svsvsvsvsv"
 OUT_BUFS = 6
+
+W_BANKS = [
+    (0, 0, 0, 0, 0),
+    (0, 0, 1, 0, 1),
+    (1, 0, 1, 1, 0),
+    (1, 1, 1, 1, 1),
+    (0, 0, 2, 2, 0),
+    (0, 0, 3, 2, 1),
+    (0, 1, 2, 3, 0),
+    (0, 1, 3, 3, 1),
+    (1, 1, 2, 4, 0),
+    (1, 1, 3, 4, 1),
+]
 
 
 def spec_range(i, rp):
@@ -123,16 +135,18 @@ def tile_cp_sparse_degree_lu_pa_t_kernel(tc, z, U_lo, masks_lo, out):
         for grp in range(1, N_GROUPS):
             load_z(grp, 0, GROUP)
 
-        def mask_mult(key):
-            i, rp = key
+        def mask_mult(i, rp):
             s0, s1 = spec_range(i, rp)
             m0, m1 = mask_range(i, rp)
-            part = raws[key][:].rearrange("p (r c) -> p r c", r=2)[:, :, m0 - s0 : m1 - s0]
+            part = raws[(i, rp)][:].rearrange("p (r c) -> p r c", r=2)[:, :, m0 - s0 : m1 - s0]
             nc.vector.tensor_tensor(
-                out=part, in0=part, in1=msks[key][:].rearrange("p (r c) -> p r c", r=2), op=ALU.mult
+                out=part, in0=part, in1=msks[(i, rp)][:].rearrange("p (r c) -> p r c", r=2), op=ALU.mult
             )
 
-        def w_bank(i, g, rp, s, half, eng):
+        held = {}
+
+        def w_transposes(n):
+            i, g, rp, s, half = W_BANKS[n]
             s0, s1 = spec_range(i, rp)
             words = (s1 - s0) // 2
             rawf = raws[(i, rp)][:].bitcast(F32)
@@ -143,10 +157,14 @@ def tile_cp_sparse_degree_lu_pa_t_kernel(tc, z, U_lo, masks_lo, out):
                     nc.tensor.transpose(
                         out=bk[:, 256 * u + P * r : 256 * u + P * r + P], in_=rawf[:, w0 : w0 + P], identity=ident[:]
                     )
+            held[("w", n)] = bk
+
+        def w_copy(n, eng):
+            i, g, rp, s, half = W_BANKS[n]
             copy_out(
                 eng,
                 wg[s][:].bitcast(F32)[:, 512 * half : 512 * half + 512].rearrange("p (r u) -> p r u", u=2),
-                bk[:].rearrange("p (u r) -> p r u", u=2),
+                held[("w", n)][:].rearrange("p (u r) -> p r u", u=2),
             )
 
         def w_quant(s):
@@ -156,27 +174,25 @@ def tile_cp_sparse_degree_lu_pa_t_kernel(tc, z, U_lo, masks_lo, out):
         zc = {}
         zs = {}
 
-        def z_tiles(grp):
-            zg[grp] = zwork.tile([P, GROUP * FEATS], BF16, name="zg%d" % grp, tag="zg", align_bytes=64)
-            zc[grp] = zwork.tile([P, GROUP * 256], U32, name="zc%d" % grp, tag="zc", align_bytes=64)
-            zs[grp] = zwork.tile([P, GROUP * 256], U8, name="zs%d" % grp, tag="zs", align_bytes=64)
-
-        def z_transposes(grp, js):
+        def z_transposes(grp, j):
+            if j == 0:
+                zg[grp] = zwork.tile([P, GROUP * FEATS], BF16, name="zg%d" % grp, tag="zg", align_bytes=64)
+                zc[grp] = zwork.tile([P, GROUP * 256], U32, name="zc%d" % grp, tag="zc", align_bytes=64)
+                zs[grp] = zwork.tile([P, GROUP * 256], U8, name="zs%d" % grp, tag="zs", align_bytes=64)
             zrf = zraw[grp][:].bitcast(F32)
-            bks = []
-            for j in js:
-                bk = bank()
-                for c in range(4):
-                    nc.tensor.transpose(
-                        out=bk[:, P * c : P * c + P], in_=zrf[:, 512 * j + P * c : 512 * j + P * c + P], identity=ident[:]
-                    )
-                bks.append(bk)
-            for j, bk in zip(js, bks):
-                copy_out(
-                    ZCOPY[j],
-                    zg[grp][:].bitcast(F32)[:, 512 * j : 512 * j + 512].rearrange("p (g t u) -> p g t u", g=2, u=2),
-                    bk[:].rearrange("p (g u t) -> p g t u", g=2, u=2),
+            bk = bank()
+            for c in range(4):
+                nc.tensor.transpose(
+                    out=bk[:, P * c : P * c + P], in_=zrf[:, 512 * j + P * c : 512 * j + P * c + P], identity=ident[:]
                 )
+            held[("z", grp, j)] = bk
+
+        def z_copy(grp, j, eng):
+            copy_out(
+                eng,
+                zg[grp][:].bitcast(F32)[:, 512 * j : 512 * j + 512].rearrange("p (g t u) -> p g t u", g=2, u=2),
+                held[("z", grp, j)][:].rearrange("p (g u t) -> p g t u", g=2, u=2),
+            )
 
         def z_quant(grp, h):
             nc.vector.quantize_mx(
@@ -199,9 +215,7 @@ def tile_cp_sparse_degree_lu_pa_t_kernel(tc, z, U_lo, masks_lo, out):
 
         osb = {}
 
-        def half_a(grp, h):
-            o = outp.tile([P, 2 * RANKS], F32, name="o%d%d" % (grp, h), tag="o")
-            osb[(grp, h)] = o
+        def mx_a(grp, h):
             y0 = []
             for jj in range(2):
                 bk = bank()
@@ -211,15 +225,23 @@ def tile_cp_sparse_degree_lu_pa_t_kernel(tc, z, U_lo, masks_lo, out):
             for jj in range(2):
                 mm(y1[:, 256 * jj : 256 * jj + 256], grp, 2 * h + jj, 0, 1, 0, 256, True, False)
                 mm(y1[:, 256 * jj : 256 * jj + 256], grp, 2 * h + jj, 1, 1, 256, 512, False, True)
+            held[("a", grp, h)] = (y0, y1)
+
+        def out_a_scalar(grp, h):
+            o = outp.tile([P, 2 * RANKS], F32, name="o%d%d" % (grp, h), tag="o")
+            osb[(grp, h)] = o
+            y0, y1 = held[("a", grp, h)]
             for jj in range(2):
                 nc.scalar.copy(out=o[:, RANKS * jj : RANKS * jj + 512], in_=y0[jj][:])
-            o3 = o[:].rearrange("p (j r) -> p j r", j=2)[:, :, 256:512]
+
+        def out_a_vector(grp, h):
+            y0, y1 = held[("a", grp, h)]
+            o3 = osb[(grp, h)][:].rearrange("p (j r) -> p j r", j=2)[:, :, 256:512]
             nc.vector.scalar_tensor_tensor(
                 out=o3, in0=y1[:].rearrange("p (j r) -> p j r", j=2), scalar=1.0, in1=o3, op0=ALU.add, op1=ALU.mult
             )
 
-        def half_b(grp, h, fine):
-            o = osb[(grp, h)]
+        def mx_b(grp, h):
             y0 = []
             for jj in range(2):
                 bk = bank()
@@ -231,8 +253,22 @@ def tile_cp_sparse_degree_lu_pa_t_kernel(tc, z, U_lo, masks_lo, out):
                 bk = bank()
                 mm(bk[:], grp, 2 * h + jj, 1, 4, 0, 512, True, True)
                 y1.append(bk)
+            held[("b", grp, h)] = (y0, y1)
+
+        def out_b_scalar(grp, h):
+            o = osb[(grp, h)]
+            y0, y1 = held[("b", grp, h)]
             for jj in range(2):
                 nc.scalar.copy(out=o[:, RANKS * jj + 512 : RANKS * jj + 1024], in_=y0[jj][:])
+
+        def store(grp, h, j0, j1, r0, r1):
+            dst = out[512 * grp : 512 * grp + 512, :].rearrange("(p j) r -> p j r", j=GROUP)
+            src = osb[(grp, h)][:].rearrange("p (j r) -> p j r", j=2)
+            nc.sync.dma_start(out=dst[:, 2 * h + j0 : 2 * h + j1, r0:r1], in_=src[:, j0:j1, r0:r1])
+
+        def out_b_vector(grp, h, fine):
+            o = osb[(grp, h)]
+            y0, y1 = held[("b", grp, h)]
             for jj in range(2):
                 part = o[:, RANKS * jj + 512 : RANKS * jj + 1024]
                 nc.vector.scalar_tensor_tensor(
@@ -243,53 +279,80 @@ def tile_cp_sparse_degree_lu_pa_t_kernel(tc, z, U_lo, masks_lo, out):
             if not fine:
                 store(grp, h, 0, 2, 0, RANKS)
 
-        def store(grp, h, j0, j1, r0, r1):
-            dst = out[512 * grp : 512 * grp + 512, :].rearrange("(p j) r -> p j r", j=GROUP)
-            src = osb[(grp, h)][:].rearrange("p (j r) -> p j r", j=2)
-            nc.sync.dma_start(out=dst[:, 2 * h + j0 : 2 * h + j1, r0:r1], in_=src[:, j0:j1, r0:r1])
-
-        for key in pairs_a:
-            mask_mult(key)
-        w_bank(0, 0, 0, 0, 0, WCOPY[0])
-        w_bank(0, 0, 1, 0, 1, WCOPY[1])
-        w_bank(1, 0, 1, 1, 0, WCOPY[2])
-        w_bank(1, 1, 1, 1, 1, WCOPY[3])
+        mask_mult(0, 0)
+        w_transposes(0)
+        w_copy(0, "s")
+        mask_mult(0, 1)
+        w_transposes(1)
+        w_copy(1, "s")
+        mask_mult(1, 1)
+        w_transposes(2)
+        w_transposes(3)
+        w_copy(2, "s")
         w_quant(0)
-        z_tiles(0)
-        z_transposes(0, [0, 1])
+        w_copy(3, "v")
+        z_transposes(0, 0)
+        z_transposes(0, 1)
+        z_copy(0, 0, "s")
+        z_copy(0, 1, "s")
         w_quant(1)
-        z_transposes(0, [2, 3])
+        z_transposes(0, 2)
+        z_transposes(0, 3)
         z_quant(0, 0)
+        z_copy(0, 2, "s")
+        z_copy(0, 3, "v")
+        mx_a(0, 0)
+        mask_mult(0, 2)
         z_quant(0, 1)
-        half_a(0, 0)
-        half_a(0, 1)
-        for key in pairs_b:
-            mask_mult(key)
-        w_bank(0, 0, 2, 2, 0, WCOPY[4])
-        w_bank(0, 0, 3, 2, 1, WCOPY[5])
-        w_bank(0, 1, 2, 3, 0, WCOPY[6])
-        w_bank(0, 1, 3, 3, 1, WCOPY[7])
+        mask_mult(0, 3)
+        out_a_scalar(0, 0)
+        mx_a(0, 1)
+        out_a_vector(0, 0)
+        mask_mult(1, 2)
+        mask_mult(1, 3)
+        out_a_scalar(0, 1)
+        for n in range(4, 10):
+            w_transposes(n)
+        out_a_vector(0, 1)
+        w_copy(4, "v")
+        w_copy(5, "s")
+        w_copy(6, "v")
+        w_copy(7, "s")
         w_quant(2)
-        w_bank(1, 1, 2, 4, 0, WCOPY[8])
-        w_bank(1, 1, 3, 4, 1, WCOPY[9])
+        w_copy(8, "s")
+        w_copy(9, "v")
         w_quant(3)
-        z_tiles(1)
-        z_transposes(1, [0, 1, 2, 3])
+        for j in range(GROUP):
+            z_transposes(1, j)
+        z_copy(1, 0, "s")
+        z_copy(1, 1, "s")
         w_quant(4)
+        z_copy(1, 2, "s")
+        z_copy(1, 3, "v")
         z_quant(1, 0)
-        half_b(0, 0, False)
+        mx_b(0, 0)
+        out_b_scalar(0, 0)
+        out_b_vector(0, 0, False)
         z_quant(1, 1)
-        half_b(0, 1, False)
+        mx_b(0, 1)
+        out_b_scalar(0, 1)
+        out_b_vector(0, 1, False)
         for grp in range(1, N_GROUPS):
             nxt = grp + 1
             if nxt < N_GROUPS:
-                z_tiles(nxt)
-                z_transposes(nxt, [0, 1, 2, 3])
+                for j in range(GROUP):
+                    z_transposes(nxt, j)
+                for j in range(GROUP):
+                    z_copy(nxt, j, ZCOPY[j])
             for h in range(2):
                 last = grp == N_GROUPS - 1 and h == 1
-                half_a(grp, h)
+                mx_a(grp, h)
+                out_a_scalar(grp, h)
+                out_a_vector(grp, h)
                 if last:
                     store(grp, h, 0, 2, 0, 512)
-                half_b(grp, h, last)
+                mx_b(grp, h)
+                out_b_scalar(grp, h)
+                out_b_vector(grp, h, last)
                 if nxt < N_GROUPS:
                     z_quant(nxt, h)

@@ -24,6 +24,8 @@ GENERAL = False
 PIN = True
 ZCOPY = "svsv"
 OUT_BUFS = 6
+RUN_GROUPS = 1
+FINE_PAIRS = 3
 
 W_BANKS = [
     (0, 0, 0, 0, 0),
@@ -215,144 +217,176 @@ def tile_cp_sparse_degree_lu_pa_t_kernel(tc, z, U_lo, masks_lo, out):
 
         osb = {}
 
-        def mx_a(grp, h):
-            y0 = []
+        def mx_y0a(grp, h):
             for jj in range(2):
                 bk = bank()
                 mm(bk[:], grp, 2 * h + jj, 0, 0, 0, 512, True, True)
-                y0.append(bk)
-            y1 = bank()
-            for jj in range(2):
-                mm(y1[:, 256 * jj : 256 * jj + 256], grp, 2 * h + jj, 0, 1, 0, 256, True, False)
-                mm(y1[:, 256 * jj : 256 * jj + 256], grp, 2 * h + jj, 1, 1, 256, 512, False, True)
-            held[("a", grp, h)] = (y0, y1)
+                held[("y0a", grp, h, jj)] = bk
 
-        def out_a_scalar(grp, h):
+        def mx_y1a(grp, h):
+            bk = bank()
+            for jj in range(2):
+                mm(bk[:, 256 * jj : 256 * jj + 256], grp, 2 * h + jj, 0, 1, 0, 256, True, False)
+                mm(bk[:, 256 * jj : 256 * jj + 256], grp, 2 * h + jj, 1, 1, 256, 512, False, True)
+            held[("y1a", grp, h)] = bk
+
+        def mx_y0b(grp, h, jj):
+            bk = bank()
+            mm(bk[:], grp, 2 * h + jj, 0, 2, 0, 512, True, False)
+            mm(bk[:], grp, 2 * h + jj, 1, 3, 0, 512, False, True)
+            held[("y0b", grp, h, jj)] = bk
+
+        def mx_y1b(grp, h, jj):
+            bk = bank()
+            mm(bk[:], grp, 2 * h + jj, 1, 4, 0, 512, True, True)
+            held[("y1b", grp, h, jj)] = bk
+
+        def out_y0a(grp, h):
             o = outp.tile([P, 2 * RANKS], F32, name="o%d%d" % (grp, h), tag="o")
             osb[(grp, h)] = o
-            y0, y1 = held[("a", grp, h)]
             for jj in range(2):
-                nc.scalar.copy(out=o[:, RANKS * jj : RANKS * jj + 512], in_=y0[jj][:])
+                nc.scalar.copy(out=o[:, RANKS * jj : RANKS * jj + 512], in_=held[("y0a", grp, h, jj)][:])
 
-        def out_a_vector(grp, h):
-            y0, y1 = held[("a", grp, h)]
+        def out_y1a(grp, h):
             o3 = osb[(grp, h)][:].rearrange("p (j r) -> p j r", j=2)[:, :, 256:512]
             nc.vector.scalar_tensor_tensor(
-                out=o3, in0=y1[:].rearrange("p (j r) -> p j r", j=2), scalar=1.0, in1=o3, op0=ALU.add, op1=ALU.mult
+                out=o3,
+                in0=held[("y1a", grp, h)][:].rearrange("p (j r) -> p j r", j=2),
+                scalar=1.0,
+                in1=o3,
+                op0=ALU.add,
+                op1=ALU.mult,
             )
 
-        def mx_b(grp, h):
-            y0 = []
-            for jj in range(2):
-                bk = bank()
-                mm(bk[:], grp, 2 * h + jj, 0, 2, 0, 512, True, False)
-                mm(bk[:], grp, 2 * h + jj, 1, 3, 0, 512, False, True)
-                y0.append(bk)
-            y1 = []
-            for jj in range(2):
-                bk = bank()
-                mm(bk[:], grp, 2 * h + jj, 1, 4, 0, 512, True, True)
-                y1.append(bk)
-            held[("b", grp, h)] = (y0, y1)
+        def out_y0b(grp, h, jj):
+            nc.scalar.copy(
+                out=osb[(grp, h)][:, RANKS * jj + 512 : RANKS * jj + 1024], in_=held[("y0b", grp, h, jj)][:]
+            )
 
-        def out_b_scalar(grp, h):
-            o = osb[(grp, h)]
-            y0, y1 = held[("b", grp, h)]
-            for jj in range(2):
-                nc.scalar.copy(out=o[:, RANKS * jj + 512 : RANKS * jj + 1024], in_=y0[jj][:])
+        def out_y1b(grp, h, jj):
+            part = osb[(grp, h)][:, RANKS * jj + 512 : RANKS * jj + 1024]
+            nc.vector.scalar_tensor_tensor(
+                out=part, in0=held[("y1b", grp, h, jj)][:], scalar=1.0, in1=part, op0=ALU.add, op1=ALU.mult
+            )
 
         def store(grp, h, j0, j1, r0, r1):
             dst = out[512 * grp : 512 * grp + 512, :].rearrange("(p j) r -> p j r", j=GROUP)
             src = osb[(grp, h)][:].rearrange("p (j r) -> p j r", j=2)
             nc.sync.dma_start(out=dst[:, 2 * h + j0 : 2 * h + j1, r0:r1], in_=src[:, j0:j1, r0:r1])
 
-        def out_b_vector(grp, h, fine):
-            o = osb[(grp, h)]
-            y0, y1 = held[("b", grp, h)]
+        def store_pair(grp, h):
+            store(grp, h, 0, 2, 0, RANKS)
+
+        def pair(grp, h):
+            fine = 2 * (N_GROUPS - 1 - grp) + (1 - h) < FINE_PAIRS
+            mx_y0a(grp, h)
+            mx_y1a(grp, h)
+            out_y0a(grp, h)
+            out_y1a(grp, h)
+            if fine:
+                store(grp, h, 0, 2, 0, 512)
             for jj in range(2):
-                part = o[:, RANKS * jj + 512 : RANKS * jj + 1024]
-                nc.vector.scalar_tensor_tensor(
-                    out=part, in0=y1[jj][:], scalar=1.0, in1=part, op0=ALU.add, op1=ALU.mult
-                )
+                mx_y0b(grp, h, jj)
+            for jj in range(2):
+                mx_y1b(grp, h, jj)
+            for jj in range(2):
+                out_y0b(grp, h, jj)
+            for jj in range(2):
+                out_y1b(grp, h, jj)
                 if fine:
                     store(grp, h, jj, jj + 1, 512, RANKS)
             if not fine:
-                store(grp, h, 0, 2, 0, RANKS)
+                store_pair(grp, h)
 
         mask_mult(0, 0)
         w_transposes(0)
-        w_copy(0, "s")
         mask_mult(0, 1)
-        w_transposes(1)
-        w_copy(1, "s")
+        w_copy(0, "v")
         mask_mult(1, 1)
+        w_transposes(1)
         w_transposes(2)
         w_transposes(3)
+        w_copy(1, "s")
         w_copy(2, "s")
         w_quant(0)
-        w_copy(3, "v")
         z_transposes(0, 0)
         z_transposes(0, 1)
+        z_copy(0, 1, "v")
         z_copy(0, 0, "s")
-        z_copy(0, 1, "s")
-        w_quant(1)
+        w_copy(3, "s")
         z_transposes(0, 2)
         z_transposes(0, 3)
         z_quant(0, 0)
+        w_quant(1)
         z_copy(0, 2, "s")
-        z_copy(0, 3, "v")
-        mx_a(0, 0)
+        z_copy(0, 3, "s")
         mask_mult(0, 2)
+        mx_y0a(0, 0)
+        mx_y1a(0, 0)
         z_quant(0, 1)
+        out_y0a(0, 0)
         mask_mult(0, 3)
-        out_a_scalar(0, 0)
-        mx_a(0, 1)
-        out_a_vector(0, 0)
+        out_y1a(0, 0)
+        mx_y0a(0, 1)
+        mx_y1a(0, 1)
+        out_y0a(0, 1)
         mask_mult(1, 2)
         mask_mult(1, 3)
-        out_a_scalar(0, 1)
-        for n in range(4, 10):
-            w_transposes(n)
-        out_a_vector(0, 1)
-        w_copy(4, "v")
-        w_copy(5, "s")
-        w_copy(6, "v")
-        w_copy(7, "s")
+        w_transposes(4)
+        w_transposes(5)
+        w_transposes(6)
+        w_transposes(7)
+        w_transposes(8)
+        w_transposes(9)
+        out_y1a(0, 1)
+        w_copy(4, "s")
+        w_copy(5, "v")
+        w_copy(6, "s")
+        w_copy(7, "v")
         w_quant(2)
         w_copy(8, "s")
-        w_copy(9, "v")
+        w_copy(9, "s")
         w_quant(3)
-        for j in range(GROUP):
-            z_transposes(1, j)
-        z_copy(1, 0, "s")
-        z_copy(1, 1, "s")
+        z_transposes(1, 0)
+        z_transposes(1, 1)
+        z_transposes(1, 2)
+        z_transposes(1, 3)
         w_quant(4)
+        z_copy(1, 0, "s")
+        z_copy(1, 1, "v")
         z_copy(1, 2, "s")
         z_copy(1, 3, "v")
+        mx_y0b(0, 0, 0)
+        mx_y0b(0, 0, 1)
+        mx_y1b(0, 0, 0)
+        mx_y1b(0, 0, 1)
+        out_y0b(0, 0, 0)
+        out_y0b(0, 0, 1)
         z_quant(1, 0)
-        mx_b(0, 0)
-        out_b_scalar(0, 0)
-        out_b_vector(0, 0, False)
+        out_y1b(0, 0, 0)
+        out_y1b(0, 0, 1)
+        store_pair(0, 0)
+        mx_y0b(0, 1, 0)
+        mx_y0b(0, 1, 1)
+        mx_y1b(0, 1, 0)
+        mx_y1b(0, 1, 1)
+        out_y0b(0, 1, 0)
+        out_y0b(0, 1, 1)
         z_quant(1, 1)
-        mx_b(0, 1)
-        out_b_scalar(0, 1)
-        out_b_vector(0, 1, False)
-        for grp in range(1, N_GROUPS):
-            nxt = grp + 1
-            if nxt < N_GROUPS:
+        out_y1b(0, 1, 0)
+        out_y1b(0, 1, 1)
+        store_pair(0, 1)
+        for first in range(1, N_GROUPS, RUN_GROUPS):
+            ahead = [g for g in range(first + 1, first + 1 + RUN_GROUPS) if g < N_GROUPS]
+            for g in ahead:
                 for j in range(GROUP):
-                    z_transposes(nxt, j)
+                    z_transposes(g, j)
+            for g in ahead:
                 for j in range(GROUP):
-                    z_copy(nxt, j, ZCOPY[j])
-            for h in range(2):
-                last = grp == N_GROUPS - 1 and h == 1
-                mx_a(grp, h)
-                out_a_scalar(grp, h)
-                out_a_vector(grp, h)
-                if last:
-                    store(grp, h, 0, 2, 0, 512)
-                mx_b(grp, h)
-                out_b_scalar(grp, h)
-                out_b_vector(grp, h, last)
-                if nxt < N_GROUPS:
-                    z_quant(nxt, h)
+                    z_copy(g, j, ZCOPY[j])
+            todo = [(g, h) for g in ahead for h in range(2)]
+            now = [(g, h) for g in range(first, first + RUN_GROUPS) if g < N_GROUPS for h in range(2)]
+            for k in range(len(now)):
+                pair(now[k][0], now[k][1])
+                if k < len(todo):
+                    z_quant(todo[k][0], todo[k][1])

@@ -24,7 +24,7 @@ GENERAL = False
 PIN = True
 ZCOPY = "svsv"
 OUT_BUFS = 6
-RUN_GROUPS = 1
+RUN_GROUPS = 2
 FINE_PAIRS = 3
 
 W_BANKS = [

@@ -67,7 +67,7 @@ def tile_cp_sparse_degree_lu_pa_t_kernel(tc, z, U_lo, masks_lo, out):
         zin = ctx.enter_context(tc.tile_pool(name="zin", bufs=N_GROUPS))
         zwork = ctx.enter_context(tc.tile_pool(name="zwork", bufs=3))
         outp = ctx.enter_context(tc.tile_pool(name="outp", bufs=OUT_BUFS))
-        psum = ctx.enter_context(tc.psum_pool(name="psum", bufs=8))
+        psum = ctx.enter_context(tc.psum_pool(name="psum", bufs=1))
         if PIN:
             ctx.enter_context(tc.manual_schedule())
 
@@ -75,7 +75,7 @@ def tile_cp_sparse_degree_lu_pa_t_kernel(tc, z, U_lo, masks_lo, out):
 
         def bank():
             count[0] += 1
-            return psum.tile([P, 512], F32, name="bank%d" % count[0], tag="bank")
+            return psum.tile([P, 512], F32, name="bank%d" % count[0], tag="bank%d" % (count[0] % 8))
 
         def copy_out(eng, dst, src):
             if eng == "s":

from contextlib import ExitStack

import concourse.mybir as mybir
from concourse.masks import make_identity

F32 = mybir.dt.float32
BF16 = mybir.dt.bfloat16
U32 = mybir.dt.uint32
U8 = mybir.dt.uint8
FP8X4 = mybir.dt.float8_e4m3fn_x4
ALU = mybir.AluOpType

P = 128
TOKENS = 4096
FEATS = 1024
RANKS = 1024
GROUP = 4
N_GROUPS = TOKENS // (P * GROUP)

FLOPS = 2 * TOKENS * 1310720
BYTES = TOKENS * FEATS * 2 + TOKENS * RANKS * 4 + 2 * 1310720 * 2

GENERAL = False
PIN = True
ZCOPY = "svsv"
OUT_BUFS = 6
RUN_GROUPS = 2
FINE_PAIRS = 3

W_BANKS = [
    (0, 0, 0, 0, 0),
    (0, 0, 1, 0, 1),
    (1, 0, 1, 1, 0),
    (1, 1, 1, 1, 1),
    (0, 0, 2, 2, 0),
    (0, 0, 3, 2, 1),
    (0, 1, 2, 3, 0),
    (0, 1, 3, 3, 1),
    (1, 1, 2, 4, 0),
    (1, 1, 3, 4, 1),
]


def spec_range(i, rp):
    if i == 0:
        return (0, 512) if rp < 2 else (0, 1024)
    return (0, 1024) if rp == 1 else (512, 1024)


def live_range(i, rp):
    if GENERAL:
        return spec_range(i, rp)
    return (0, 256 * (rp + 1)) if i == 0 else (256 * rp, 1024)


def mask_range(i, rp):
    if GENERAL:
        return spec_range(i, rp)
    return (256 * rp, 256 * rp + 256)


def tile_cp_sparse_degree_lu_pa_t_kernel(tc, z, U_lo, masks_lo, out):
    nc = tc.nc
    zf = z.flatten_outer_dims()
    with ExitStack() as ctx:
        const = ctx.enter_context(tc.tile_pool(name="const", bufs=1))
        zin = ctx.enter_context(tc.tile_pool(name="zin", bufs=N_GROUPS))
        zwork = ctx.enter_context(tc.tile_pool(name="zwork", bufs=3))
        outp = ctx.enter_context(tc.tile_pool(name="outp", bufs=OUT_BUFS))
        psum = ctx.enter_context(tc.psum_pool(name="psum", bufs=1))
        if PIN:
            ctx.enter_context(tc.manual_schedule())

        count = [0]

        def bank():
            count[0] += 1
            return psum.tile([P, 512], F32, name="bank%d" % count[0], tag="bank%d" % (count[0] % 8))

        def copy_out(eng, dst, src):
            if eng == "s":
                nc.scalar.copy(out=dst, in_=src)
            else:
                nc.vector.tensor_copy(out=dst, in_=src)

        ident = const.tile([P, P], F32, name="ident")
        make_identity(nc, ident[:])

        pairs_a = [(0, 0), (0, 1), (1, 1)]
        pairs_b = [(0, 2), (0, 3), (1, 2), (1, 3)]
        raws = {}
        msks = {}
        for key in pairs_a + pairs_b:
            i, rp = key
            s0, s1 = spec_range(i, rp)
            m0, m1 = mask_range(i, rp)
            raws[key] = const.tile([P, 2 * (s1 - s0)], BF16, name="raw%d%d" % key)
            msks[key] = const.tile([P, 2 * (m1 - m0)], BF16, name="msk%d%d" % key)
            l0, l1 = live_range(i, rp)
            r3 = raws[key][:].rearrange("p (r c) -> p r c", r=2)
            if l0 > s0:
                nc.vector.memset(r3[:, :, 0 : l0 - s0], 0.0)
            if l1 < s1:
                nc.vector.memset(r3[:, :, l1 - s0 : s1 - s0], 0.0)
        wg = [const.tile([P, 2048], BF16, name="wg%d" % s, align_bytes=64) for s in range(5)]
        wc = [const.tile([P, 512], U32, name="wc%d" % s, align_bytes=64) for s in range(5)]
        ws = [const.tile([P, 512], U8, name="ws%d" % s, align_bytes=64) for s in range(5)]

        def load_w(key):
            i, rp = key
            s0, s1 = spec_range(i, rp)
            m0, m1 = mask_range(i, rp)
            l0, l1 = live_range(i, rp)
            rows = slice(256 * rp, 256 * rp + 256)
            nc.sync.dma_start(
                out=msks[key][:].rearrange("p (r c) -> p r c", r=2),
                in_=masks_lo[i, rows, m0:m1].rearrange("(r p) c -> p r c", p=P),
            )
            nc.sync.dma_start(
                out=raws[key][:].rearrange("p (r c) -> p r c", r=2)[:, :, l0 - s0 : l1 - s0],
                in_=U_lo[i, rows, l0:l1].rearrange("(r p) c -> p r c", p=P),
            )

        zraw = [zin.tile([P, GROUP * FEATS], BF16, name="zraw%d" % g, tag="zraw") for g in range(N_GROUPS)]

        def load_z(grp, j0, j1):
            src = zf[512 * grp : 512 * grp + 512, :].rearrange("(p j) c -> p j c", j=GROUP)
            dst = zraw[grp][:].rearrange("p (j c) -> p j c", j=GROUP)
            nc.sync.dma_start(out=dst[:, j0:j1, :], in_=src[:, j0:j1, :])

        for key in pairs_a:
            load_w(key)
        load_z(0, 0, 2)
        load_z(0, 2, 4)
        for key in pairs_b:
            load_w(key)
        for grp in range(1, N_GROUPS):
            load_z(grp, 0, GROUP)

        def mask_mult(i, rp):
            s0, s1 = spec_range(i, rp)
            m0, m1 = mask_range(i, rp)
            part = raws[(i, rp)][:].rearrange("p (r c) -> p r c", r=2)[:, :, m0 - s0 : m1 - s0]
            nc.vector.tensor_tensor(
                out=part, in0=part, in1=msks[(i, rp)][:].rearrange("p (r c) -> p r c", r=2), op=ALU.mult
            )

        held = {}

        def w_transposes(n):
            i, g, rp, s, half = W_BANKS[n]
            s0, s1 = spec_range(i, rp)
            words = (s1 - s0) // 2
            rawf = raws[(i, rp)][:].bitcast(F32)
            bk = bank()
            for u in range(2):
                for r in range(2):
                    w0 = r * words + (512 * g + 256 * u - s0) // 2
                    nc.tensor.transpose(
                        out=bk[:, 256 * u + P * r : 256 * u + P * r + P], in_=rawf[:, w0 : w0 + P], identity=ident[:]
                    )
            held[("w", n)] = bk

        def w_copy(n, eng):
            i, g, rp, s, half = W_BANKS[n]
            copy_out(
                eng,
                wg[s][:].bitcast(F32)[:, 512 * half : 512 * half + 512].rearrange("p (r u) -> p r u", u=2),
                held[("w", n)][:].rearrange("p (u r) -> p r u", u=2),
            )

        def w_quant(s):
            nc.vector.quantize_mx(out=wc[s][:].bitcast(FP8X4), scales=ws[s][:], in_=wg[s][:])

        zg = {}
        zc = {}
        zs = {}

        def z_transposes(grp, j):
            if j == 0:
                zg[grp] = zwork.tile([P, GROUP * FEATS], BF16, name="zg%d" % grp, tag="zg", align_bytes=64)
                zc[grp] = zwork.tile([P, GROUP * 256], U32, name="zc%d" % grp, tag="zc", align_bytes=64)
                zs[grp] = zwork.tile([P, GROUP * 256], U8, name="zs%d" % grp, tag="zs", align_bytes=64)
            zrf = zraw[grp][:].bitcast(F32)
            bk = bank()
            for c in range(4):
                nc.tensor.transpose(
                    out=bk[:, P * c : P * c + P], in_=zrf[:, 512 * j + P * c : 512 * j + P * c + P], identity=ident[:]
                )
            held[("z", grp, j)] = bk

        def z_copy(grp, j, eng):
            copy_out(
                eng,
                zg[grp][:].bitcast(F32)[:, 512 * j : 512 * j + 512].rearrange("p (g t u) -> p g t u", g=2, u=2),
                held[("z", grp, j)][:].rearrange("p (g u t) -> p g t u", g=2, u=2),
            )

        def z_quant(grp, h):
            nc.vector.quantize_mx(
                out=zc[grp][:, 512 * h : 512 * h + 512].bitcast(FP8X4),
                scales=zs[grp][:, 512 * h : 512 * h + 512],
                in_=zg[grp][:, 2048 * h : 2048 * h + 2048],
            )

        def mm(dst, grp, j, g, s, c0, c1, start, stop):
            a = 256 * j + P * g
            nc.tensor.matmul_mx(
                out=dst,
                lhsT=zc[grp][:, a : a + P].bitcast(FP8X4),
                lhsT_scale=zs[grp][:, a : a + P],
                rhs=wc[s][:, c0:c1].bitcast(FP8X4),
                rhs_scale=ws[s][:, c0:c1],
                start=start,
                stop=stop,
            )

        osb = {}

        def mx_y0a(grp, h):
            for jj in range(2):
                bk = bank()
                mm(bk[:], grp, 2 * h + jj, 0, 0, 0, 512, True, True)
                held[("y0a", grp, h, jj)] = bk

        def mx_y1a(grp, h):
            bk = bank()
            for jj in range(2):
                mm(bk[:, 256 * jj : 256 * jj + 256], grp, 2 * h + jj, 0, 1, 0, 256, True, False)
                mm(bk[:, 256 * jj : 256 * jj + 256], grp, 2 * h + jj, 1, 1, 256, 512, False, True)
            held[("y1a", grp, h)] = bk

        def mx_y0b(grp, h, jj):
            bk = bank()
            mm(bk[:], grp, 2 * h + jj, 0, 2, 0, 512, True, False)
            mm(bk[:], grp, 2 * h + jj, 1, 3, 0, 512, False, True)
            held[("y0b", grp, h, jj)] = bk

        def mx_y1b(grp, h, jj):
            bk = bank()
            mm(bk[:], grp, 2 * h + jj, 1, 4, 0, 512, True, True)
            held[("y1b", grp, h, jj)] = bk

        def out_y0a(grp, h):
            o = outp.tile([P, 2 * RANKS], F32, name="o%d%d" % (grp, h), tag="o")
            osb[(grp, h)] = o
            for jj in range(2):
                nc.scalar.copy(out=o[:, RANKS * jj : RANKS * jj + 512], in_=held[("y0a", grp, h, jj)][:])

        def out_y1a(grp, h):
            o3 = osb[(grp, h)][:].rearrange("p (j r) -> p j r", j=2)[:, :, 256:512]
            nc.vector.scalar_tensor_tensor(
                out=o3,
                in0=held[("y1a", grp, h)][:].rearrange("p (j r) -> p j r", j=2),
                scalar=1.0,
                in1=o3,
                op0=ALU.add,
                op1=ALU.mult,
            )

        def out_y0b(grp, h, jj):
            nc.scalar.copy(
                out=osb[(grp, h)][:, RANKS * jj + 512 : RANKS * jj + 1024], in_=held[("y0b", grp, h, jj)][:]
            )

        def out_y1b(grp, h, jj):
            part = osb[(grp, h)][:, RANKS * jj + 512 : RANKS * jj + 1024]
            nc.vector.scalar_tensor_tensor(
                out=part, in0=held[("y1b", grp, h, jj)][:], scalar=1.0, in1=part, op0=ALU.add, op1=ALU.mult
            )

        def store(grp, h, j0, j1, r0, r1):
            dst = out[512 * grp : 512 * grp + 512, :].rearrange("(p j) r -> p j r", j=GROUP)
            src = osb[(grp, h)][:].rearrange("p (j r) -> p j r", j=2)
            nc.sync.dma_start(out=dst[:, 2 * h + j0 : 2 * h + j1, r0:r1], in_=src[:, j0:j1, r0:r1])

        def store_pair(grp, h):
            store(grp, h, 0, 2, 0, RANKS)

        def pair(grp, h):
            fine = 2 * (N_GROUPS - 1 - grp) + (1 - h) < FINE_PAIRS
            mx_y0a(grp, h)
            mx_y1a(grp, h)
            out_y0a(grp, h)
            out_y1a(grp, h)
            if fine:
                store(grp, h, 0, 2, 0, 512)
            for jj in range(2):
                mx_y0b(grp, h, jj)
            for jj in range(2):
                mx_y1b(grp, h, jj)
            for jj in range(2):
                out_y0b(grp, h, jj)
            for jj in range(2):
                out_y1b(grp, h, jj)
                if fine:
                    store(grp, h, jj, jj + 1, 512, RANKS)
            if not fine:
                store_pair(grp, h)

        mask_mult(0, 0)
        w_transposes(0)
        mask_mult(0, 1)
        w_copy(0, "v")
        mask_mult(1, 1)
        w_transposes(1)
        w_transposes(2)
        w_transposes(3)
        w_copy(1, "s")
        w_copy(2, "s")
        w_quant(0)
        z_transposes(0, 0)
        z_transposes(0, 1)
        z_copy(0, 1, "v")
        z_copy(0, 0, "s")
        w_copy(3, "s")
        z_transposes(0, 2)
        z_transposes(0, 3)
        z_quant(0, 0)
        w_quant(1)
        z_copy(0, 2, "s")
        z_copy(0, 3, "s")
        mask_mult(0, 2)
        mx_y0a(0, 0)
        mx_y1a(0, 0)
        z_quant(0, 1)
        out_y0a(0, 0)
        mask_mult(0, 3)
        out_y1a(0, 0)
        mx_y0a(0, 1)
        mx_y1a(0, 1)
        out_y0a(0, 1)
        mask_mult(1, 2)
        mask_mult(1, 3)
        w_transposes(4)
        w_transposes(5)
        w_transposes(6)
        w_transposes(7)
        w_transposes(8)
        w_transposes(9)
        out_y1a(0, 1)
        w_copy(4, "s")
        w_copy(5, "v")
        w_copy(6, "s")
        w_copy(7, "v")
        w_quant(2)
        w_copy(8, "s")
        w_copy(9, "s")
        w_quant(3)
        z_transposes(1, 0)
        z_transposes(1, 1)
        z_transposes(1, 2)
        z_transposes(1, 3)
        w_quant(4)
        z_copy(1, 0, "s")
        z_copy(1, 1, "v")
        z_copy(1, 2, "s")
        z_copy(1, 3, "v")
        mx_y0b(0, 0, 0)
        mx_y0b(0, 0, 1)
        mx_y1b(0, 0, 0)
        mx_y1b(0, 0, 1)
        out_y0b(0, 0, 0)
        out_y0b(0, 0, 1)
        z_quant(1, 0)
        out_y1b(0, 0, 0)
        out_y1b(0, 0, 1)
        store_pair(0, 0)
        mx_y0b(0, 1, 0)
        mx_y0b(0, 1, 1)
        mx_y1b(0, 1, 0)
        mx_y1b(0, 1, 1)
        out_y0b(0, 1, 0)
        out_y0b(0, 1, 1)
        z_quant(1, 1)
        out_y1b(0, 1, 0)
        out_y1b(0, 1, 1)
        store_pair(0, 1)
        for first in range(1, N_GROUPS, RUN_GROUPS):
            ahead = [g for g in range(first + 1, first + 1 + RUN_GROUPS) if g < N_GROUPS]
            for g in ahead:
                for j in range(GROUP):
                    z_transposes(g, j)
            for g in ahead:
                for j in range(GROUP):
                    z_copy(g, j, ZCOPY[j])
            todo = [(g, h) for g in ahead for h in range(2)]
            now = [(g, h) for g in range(first, first + RUN_GROUPS) if g < N_GROUPS for h in range(2)]
            for k in range(len(now)):
                pair(now[k][0], now[k][1])
                if k < len(todo):
                    z_quant(todo[k][0], todo[k][1])
